import numpy as np
import ml_dtypes


def mxq(x, axis, fmt="e4m3"):
    dtype, down = {"e4m3": (ml_dtypes.float8_e4m3fn, 7), "e5m2": (ml_dtypes.float8_e5m2, 14)}[fmt]
    v = np.moveaxis(np.asarray(x, np.float32).astype(ml_dtypes.bfloat16).astype(np.float64), axis, -1)
    blocks = v.reshape(v.shape[:-1] + (-1, 32))
    amax = np.abs(blocks).max(-1, keepdims=True)
    byte = np.maximum(np.where(amax > 0, np.frexp(amax)[1] - 1 + 127, 0) - down, 1)
    scale = np.exp2(byte - 127.0)
    codes = (blocks / scale).astype(np.float32).astype(dtype).astype(np.float64)
    return np.moveaxis((codes * scale).reshape(v.shape), -1, axis)


WIDE = False


def mx_kscale(k):
    if not WIDE:
        return np.ones(k)
    levels = np.array([30, -30])
    if k % 512:
        return np.exp2(np.random.permutation(np.resize(levels, k // 32))).repeat(32)
    a = np.empty((k // 512, 16))
    for p in range(k // 512):
        a[p, :8] = np.random.permutation(np.resize(levels, 8))
        for g in range(8):
            far = levels[np.abs(levels - a[p, g]) >= 10]
            a[p, g + 8] = far[np.random.randint(len(far))]
    return np.exp2(a.ravel()).repeat(32)


BF16 = ml_dtypes.bfloat16


def bf(x):
    return np.asarray(x, np.float32).astype(BF16)


def f64(x):
    return np.asarray(x).astype(np.float64)


B, T, C, HQ, HKV, HD = 4, 256, 2048, 16, 4, 128
EPS = 1e-6


def apply_rope(u, cos, sin):
    c = cos[None, :, None, :]
    s = sin[None, :, None, :]
    u1, u2 = u[..., ::2], u[..., 1::2]
    return np.concatenate([u1 * c - u2 * s, u1 * s + u2 * c], axis=-1)


def rmsnorm(u, w):
    return w * (u / np.sqrt(np.mean(u * u, axis=-1, keepdims=True) + EPS))


def setup_inputs():
    s = mx_kscale(C)
    inv_freq = 1.0 / (10000.0 ** (np.arange(0, HD, 2) / HD))
    freqs = np.arange(T)[:, None] * inv_freq[None, :]
    return {"x": bf(np.random.standard_normal((B, T, C)) * s),
            "Wq": bf(np.random.standard_normal((HQ * HD, C)) / np.sqrt(C) / s),
            "bq": bf(np.random.standard_normal(HQ * HD) * 0.3),
            "Wk": bf(np.random.standard_normal((HKV * HD, C)) / np.sqrt(C) / s),
            "bk": bf(np.random.standard_normal(HKV * HD) * 0.3),
            "qn_w": bf(1.0 + 0.1 * np.random.standard_normal(HD)),
            "kn_w": bf(1.0 + 0.1 * np.random.standard_normal(HD)),
            "cos": bf(np.cos(freqs)),
            "sin": bf(np.sin(freqs))}


def reference(x, Wq, bq, Wk, bk, qn_w, kn_w, cos, sin):
    xq = mxq(f64(x).reshape(B * T, C), 1, "e5m2")
    q = ((xq @ mxq(f64(Wq), 1, "e5m2").T) + f64(bq)).reshape(B, T, HQ, HD)
    k = ((xq @ mxq(f64(Wk), 1, "e5m2").T) + f64(bk)).reshape(B, T, HKV, HD)
    q = rmsnorm(apply_rope(q, f64(cos), f64(sin)), f64(qn_w))
    k = rmsnorm(apply_rope(k, f64(cos), f64(sin)), f64(kn_w))
    return q, k

@@ -1,0 +1,252 @@
+from contextlib import ExitStack
+
+import concourse.mybir as mybir
+from concourse.masks import make_identity
+
+F32 = mybir.dt.float32
+BF16 = mybir.dt.bfloat16
+U32 = mybir.dt.uint32
+U8 = mybir.dt.uint8
+E5M2X4 = mybir.dt.float8_e5m2_x4
+ALU = mybir.AluOpType
+ACT = mybir.ActivationFunctionType
+
+B, T, C, HQ, HKV, HD = 4, 256, 2048, 16, 4, 128
+EPS = 1e-6
+FLOPS = 2 * B * T * C * (HQ + HKV) * HD
+
+P = 128
+HALF = HD // 2
+PASSES = C // 512
+N_TOK = 512
+TOK_TILES = N_TOK // P
+Q_PAIRS = HQ // 2
+PAIRS = (HQ + HKV) // 2
+BANKS = 8
+BANK_COLS = 512
+RAW_BUFS = 12
+
+
+def tile_gqaselfattention_pa_kernel(tc, x, Wq, bq, Wk, bk, qn_w, kn_w, cos, sin, out_0, out_1):
+    nc = tc.nc
+    x_rows = x.rearrange("b t c -> (b t) c")
+    q_rows = out_0.rearrange("b t h d -> (b t) (h d)")
+    k_rows = out_1.rearrange("b t h d -> (b t) (h d)")
+
+    steps = [(j, 0) for j in range(3)] + [(j, 1) for j in range(3)]
+    steps += [(j, n) for j in range(3, PAIRS) for n in range(2)]
+    x_tiles = [("x", i) for i in range(2 * TOK_TILES)]
+    w_tiles = [("w", i) for i in range(2 * PAIRS)]
+    order = x_tiles[:4] + w_tiles[:6] + x_tiles[4:] + w_tiles[6:]
+    prologue_tiles = 8
+    tiles_in_step = [3, 3] + [1] * (len(order) - prologue_tiles - 6)
+    tiles_in_step += [0] * (len(steps) - len(tiles_in_step))
+
+    with ExitStack() as ctx:
+        const = ctx.enter_context(tc.tile_pool(name="const", bufs=1))
+        raw_pool = ctx.enter_context(tc.tile_pool(name="raw", bufs=RAW_BUFS))
+        work = ctx.enter_context(tc.tile_pool(name="work", bufs=2))
+        psum = ctx.enter_context(tc.psum_pool(name="psum", bufs=1))
+        ctx.enter_context(tc.manual_schedule())
+
+        bank_count = []
+
+        def next_bank():
+            index = len(bank_count) % BANKS
+            bank_count.append(index)
+            return psum.tile([P, BANK_COLS], F32, name="bank%d" % index, tag="bank%d" % index)
+
+        raw = {}
+        grouped = {}
+        x_codes = const.tile([P, 2, PASSES, N_TOK], U32, align_bytes=64)
+        x_scales = const.tile([P, 2, PASSES, N_TOK], U8, align_bytes=64)
+        w_codes = {}
+        w_scales = {}
+
+        def load(key):
+            kind, i = key
+            rows = raw_pool.tile([P, C], BF16, name="rows", tag="rows")
+            if kind == "x":
+                source = x_rows[i * P : (i + 1) * P, :]
+            else:
+                j, e = divmod(i, 2)
+                weight, first = (Wq, j * 2 * P) if j < Q_PAIRS else (Wk, (j - Q_PAIRS) * 2 * P)
+                source = weight[first : first + 2 * P, :].rearrange("(p e) c -> p e c", e=2)[:, e, :]
+            nc.sync.dma_start(out=rows[:], in_=source)
+            raw[key] = rows
+
+        def transpose_in(key):
+            words = raw[key][:].bitcast(F32)
+            side_by_side = work.tile([P, PASSES, P, 2], F32, name="grouped", tag="grouped", bufs=5, align_bytes=64)
+            for g0 in range(0, PASSES, 2):
+                bank = next_bank()
+                slots = bank[:].rearrange("p (g u r) -> p g u r", g=2, u=2)
+                for g in range(2):
+                    for u in range(2):
+                        first = 2 * P * (g0 + g)
+                        nc.tensor.transpose(slots[:, g, u, :], words[:, first + u : first + 2 * P : 2], identity[:])
+                nc.scalar.copy(out=side_by_side[:, g0 : g0 + 2, :, :], in_=slots.rearrange("p g u r -> p g r u"))
+            grouped[key] = side_by_side
+
+        def quantize(key):
+            kind, i = key
+            values = grouped[key][:].rearrange("p g r u -> p (g r u)").bitcast(BF16)
+            if kind == "x":
+                n, tt = divmod(i, TOK_TILES)
+                cols = slice(tt * P, (tt + 1) * P)
+                for g in range(PASSES):
+                    nc.vector.quantize_mx(
+                        out=x_codes[:, n, g, cols].bitcast(E5M2X4),
+                        scales=x_scales[:, n, g, cols],
+                        in_=values[:, g * 4 * P : (g + 1) * 4 * P],
+                    )
+            else:
+                codes = work.tile([P, PASSES * P], U32, name="w_codes", tag="w_codes", bufs=10, align_bytes=64)
+                scales = work.tile([P, PASSES * P], U8, name="w_scales", tag="w_scales", bufs=10, align_bytes=64)
+                nc.vector.quantize_mx(out=codes[:].bitcast(E5M2X4), scales=scales[:], in_=values)
+                w_codes[i] = codes
+                w_scales[i] = scales
+
+        def project(j, e, n):
+            bank = next_bank()
+            for g in range(PASSES):
+                cols = slice(g * P, (g + 1) * P)
+                nc.tensor.matmul_mx(
+                    out=bank[:],
+                    lhsT=w_codes[2 * j + e][:, cols].bitcast(E5M2X4),
+                    lhsT_scale=w_scales[2 * j + e][:, cols],
+                    rhs=x_codes[:, n, g, :].bitcast(E5M2X4),
+                    rhs_scale=x_scales[:, n, g, :],
+                    start=(g == 0),
+                    stop=(g == PASSES - 1),
+                )
+            return bank
+
+        def times_table(bank, j, e, which):
+            product = work.tile([P, N_TOK], F32, name="product", tag="product%d%d" % (e, which))
+            nc.vector.scalar_tensor_tensor(
+                out=product[:].rearrange("p (b t) -> p b t", t=T),
+                in0=bank[:].rearrange("p (b t) -> p b t", t=T),
+                scalar=bias[:, 2 * j + e : 2 * j + e + 1],
+                in1=tables[:, which : which + 1, :].to_broadcast([P, N_TOK // T, T]),
+                op0=ALU.add,
+                op1=ALU.mult,
+            )
+            return product
+
+        def finish(j, n, rotated):
+            gain = gains[:, 0 if j < Q_PAIRS else 1, :].rearrange("p (f i) -> p f i", f=2)
+            result = work.tile([P, TOK_TILES, 2, 2, HALF], F32, name="result", tag="result", bufs=4)
+            banks = []
+            for tt0 in range(0, TOK_TILES, 2):
+                bank = next_bank()
+                slots = bank[:].rearrange("p (t f c) -> p t f c", t=2, f=2)
+                for t in range(2):
+                    for f in range(2):
+                        cols = slice((tt0 + t) * P, (tt0 + t + 1) * P)
+                        nc.tensor.transpose(slots[:, t, f, :], rotated[f][:, cols], identity[:])
+                banks.append(bank[:].rearrange("p (t f h i) -> p t h f i", t=2, f=2, h=2))
+            scales = []
+            for heads in banks:
+                squares = work.tile([P, 2, 2, 2, HALF], BF16, name="squares", tag="squares", bufs=3)
+                sums = work.tile([P, 4], F32, name="sums", tag="sums", bufs=4)
+                for t in range(2):
+                    for h in range(2):
+                        nc.scalar.activation(
+                            out=squares[:, t, h, :, :],
+                            in_=heads[:, t, h, :, :],
+                            func=ACT.Square,
+                            accum_out=sums[:, 2 * t + h : 2 * t + h + 1],
+                        )
+                inverse_rms = work.tile([P, 4], F32, name="inverse_rms", tag="inverse_rms", bufs=4)
+                nc.scalar.activation(out=inverse_rms[:], in_=sums[:], func=ACT.Abs_reciprocal_sqrt, scale=1.0 / HD, bias=EPS)
+                scales.append(inverse_rms)
+            for half in range(2):
+                for t in range(2):
+                    for h in range(2):
+                        nc.vector.scalar_tensor_tensor(
+                            out=result[:, 2 * half + t, h, :, :],
+                            in0=banks[half][:, t, h, :, :],
+                            scalar=scales[half][:, 2 * t + h : 2 * t + h + 1],
+                            in1=gain,
+                            op0=ALU.mult,
+                            op1=ALU.mult,
+                        )
+            rows, first = (q_rows, j * 2 * HD) if j < Q_PAIRS else (k_rows, (j - Q_PAIRS) * 2 * HD)
+            target = rows[n * N_TOK : (n + 1) * N_TOK, first : first + 2 * HD]
+            nc.sync.dma_start(
+                out=target.rearrange("(t p) c -> p t c", p=P),
+                in_=result[:].rearrange("p t h f i -> p t (h f i)"),
+            )
+
+        for key in order[:RAW_BUFS]:
+            load(key)
+        loaded = RAW_BUFS
+
+        identity = const.tile([P, P], F32)
+        make_identity(nc, identity[:])
+
+        angles = const.tile([P, 2, 2, HALF], BF16)
+        nc.scalar.dma_start(out=angles[:, 0, :, :], in_=cos.rearrange("(s p) i -> p s i", p=P))
+        nc.scalar.dma_start(out=angles[:, 1, :, :], in_=sin.rearrange("(s p) i -> p s i", p=P))
+        bias_rows = const.tile([P, 2 * P], BF16)
+        nc.vector.memset(bias_rows[:], 0.0)
+        nc.scalar.dma_start(out=bias_rows[0:Q_PAIRS, :], in_=bq.rearrange("(j c) -> j c", c=2 * P))
+        nc.scalar.dma_start(out=bias_rows[Q_PAIRS:PAIRS, :], in_=bk.rearrange("(j c) -> j c", c=2 * P))
+        gains = const.tile([P, 2, HD], BF16)
+        nc.scalar.dma_start(out=gains[:, 0, :], in_=qn_w.partition_broadcast(P))
+        nc.scalar.dma_start(out=gains[:, 1, :], in_=kn_w.partition_broadcast(P))
+
+        doubled = const.tile([P, 4, 2, HALF], F32)
+        nc.vector.tensor_copy(
+            out=doubled[:],
+            in_=angles[:].rearrange("p w s i -> p (w s) i").unsqueeze(2).to_broadcast([P, 4, 2, HALF]),
+        )
+        tables = const.tile([P, 2, T], F32)
+        bias = const.tile([P, 2 * PAIRS], F32)
+
+        def transpose_constants():
+            bank = next_bank()
+            for s in range(4):
+                nc.tensor.transpose(bank[:, s * P : (s + 1) * P], doubled[:, s, :, :].rearrange("p h i -> p (h i)"), identity[:])
+            nc.vector.tensor_copy(out=tables[:].rearrange("p w t -> p (w t)"), in_=bank[:])
+            bank = next_bank()
+            nc.tensor.transpose(bank[:, 0:P], bias_rows[:].bitcast(F32), identity[:])
+            nc.vector.tensor_copy(out=bias[:], in_=bank[:, 0:PAIRS].bitcast(BF16))
+
+        for position, key in enumerate(order[:prologue_tiles]):
+            transpose_in(key)
+            if position == 1:
+                transpose_constants()
+            if position > 0:
+                quantize(order[position - 1])
+            load(order[loaded])
+            loaded += 1
+        waiting = [order[prologue_tiles - 1]]
+        done = prologue_tiles
+
+        previous = None
+        for k, (j, n) in enumerate(steps):
+            even = project(j, 0, n)
+            odd = project(j, 1, n)
+            even_cos = times_table(even, j, 0, 0)
+            even_sin = times_table(even, j, 0, 1)
+            for key in waiting:
+                quantize(key)
+            odd_sin = times_table(odd, j, 1, 1)
+            odd_cos = times_table(odd, j, 1, 0)
+            first_half = work.tile([P, N_TOK], F32, name="first_half", tag="first_half")
+            second_half = work.tile([P, N_TOK], F32, name="second_half", tag="second_half")
+            nc.gpsimd.tensor_tensor(out=first_half[:], in0=even_cos[:], in1=odd_sin[:], op=ALU.subtract)
+            nc.gpsimd.tensor_tensor(out=second_half[:], in0=even_sin[:], in1=odd_cos[:], op=ALU.add)
+            if previous is not None:
+                finish(*previous)
+            previous = (j, n, (first_half, second_half))
+            waiting = order[done : done + tiles_in_step[k]]
+            done += tiles_in_step[k]
+            for key in waiting:
+                transpose_in(key)
+                if loaded < len(order):
+                    load(order[loaded])
+                    loaded += 1
+        finish(*previous)

@@ -19,12 +19,14 @@ P = 128
 HALF = HD // 2
 PASSES = C // 512
 N_TOK = 512
-TOK_TILES = N_TOK // P
 Q_PAIRS = HQ // 2
 PAIRS = (HQ + HKV) // 2
 BANKS = 8
 BANK_COLS = 512
 RAW_BUFS = 12
+EARLY_PAIRS = 3
+LAG = 2
+TILES_ON_SCALAR = 2
 
 
 def tile_gqaselfattention_pa_kernel(tc, x, Wq, bq, Wk, bk, qn_w, kn_w, cos, sin, out_0, out_1):
@@ -33,13 +35,15 @@ def tile_gqaselfattention_pa_kernel(tc, x, Wq, bq, Wk, bk, qn_w, kn_w, cos, sin,
     q_rows = out_0.rearrange("b t h d -> (b t) (h d)")
     k_rows = out_1.rearrange("b t h d -> (b t) (h d)")
 
-    steps = [(j, 0) for j in range(3)] + [(j, 1) for j in range(3)]
-    steps += [(j, n) for j in range(3, PAIRS) for n in range(2)]
-    x_tiles = [("x", i) for i in range(2 * TOK_TILES)]
+    steps = [(0, 0, T), (0, T, T)] + [(j, 0, N_TOK) for j in range(1, EARLY_PAIRS)]
+    steps += [(j, N_TOK, N_TOK) for j in range(EARLY_PAIRS)]
+    steps += [(j, first, N_TOK) for j in range(EARLY_PAIRS, PAIRS) for first in (0, N_TOK)]
+    steps = steps[:-1] + [(PAIRS - 1, N_TOK, T), (PAIRS - 1, N_TOK + T, T)]
+    x_tiles = [("x", i) for i in range(2 * B)]
     w_tiles = [("w", i) for i in range(2 * PAIRS)]
-    order = x_tiles[:4] + w_tiles[:6] + x_tiles[4:] + w_tiles[6:]
-    prologue_tiles = 8
-    tiles_in_step = [3, 3] + [1] * (len(order) - prologue_tiles - 6)
+    order = x_tiles[:2] + w_tiles[:2] + x_tiles[2:4] + w_tiles[2 : 2 * EARLY_PAIRS] + x_tiles[4:] + w_tiles[2 * EARLY_PAIRS :]
+    prologue_tiles = 6
+    tiles_in_step = [2, 2, 4] + [1] * (2 * (PAIRS - EARLY_PAIRS))
     tiles_in_step += [0] * (len(steps) - len(tiles_in_step))
 
     with ExitStack() as ctx:
@@ -49,17 +53,18 @@ def tile_gqaselfattention_pa_kernel(tc, x, Wq, bq, Wk, bk, qn_w, kn_w, cos, sin,
         psum = ctx.enter_context(tc.psum_pool(name="psum", bufs=1))
         ctx.enter_context(tc.manual_schedule())
 
-        bank_count = []
+        banks_taken = []
 
         def next_bank():
-            index = len(bank_count) % BANKS
-            bank_count.append(index)
+            index = len(banks_taken) % BANKS
+            banks_taken.append(index)
             return psum.tile([P, BANK_COLS], F32, name="bank%d" % index, tag="bank%d" % index)
 
         raw = {}
-        grouped = {}
-        x_codes = const.tile([P, 2, PASSES, N_TOK], U32, align_bytes=64)
-        x_scales = const.tile([P, 2, PASSES, N_TOK], U8, align_bytes=64)
+        x_grouped = {}
+        w_grouped = {}
+        x_codes = const.tile([P, PASSES, B * T], U32, align_bytes=64)
+        x_scales = const.tile([P, PASSES, B * T], U8, align_bytes=64)
         w_codes = {}
         w_scales = {}
 
@@ -76,8 +81,17 @@ def tile_gqaselfattention_pa_kernel(tc, x, Wq, bq, Wk, bk, qn_w, kn_w, cos, sin,
             raw[key] = rows
 
         def transpose_in(key):
+            kind, i = key
             words = raw[key][:].bitcast(F32)
-            side_by_side = work.tile([P, PASSES, P, 2], F32, name="grouped", tag="grouped", bufs=5, align_bytes=64)
+            if kind == "w":
+                w_grouped[i] = work.tile([P, PASSES, P, 2], F32, name="w_grouped", tag="w_grouped", bufs=3, align_bytes=64)
+                side_by_side = w_grouped[i][:]
+            else:
+                b, s = divmod(i, 2)
+                if s == 0:
+                    x_grouped[b] = work.tile([P, PASSES, T, 2], F32, name="x_grouped", tag="x_grouped", align_bytes=64)
+                side_by_side = x_grouped[b][:, :, s * P : (s + 1) * P, :]
+            copies = []
             for g0 in range(0, PASSES, 2):
                 bank = next_bank()
                 slots = bank[:].rearrange("p (g u r) -> p g u r", g=2, u=2)
@@ -85,104 +99,134 @@ def tile_gqaselfattention_pa_kernel(tc, x, Wq, bq, Wk, bk, qn_w, kn_w, cos, sin,
                     for u in range(2):
                         first = 2 * P * (g0 + g)
                         nc.tensor.transpose(slots[:, g, u, :], words[:, first + u : first + 2 * P : 2], identity[:])
-                nc.scalar.copy(out=side_by_side[:, g0 : g0 + 2, :, :], in_=slots.rearrange("p g u r -> p g r u"))
-            grouped[key] = side_by_side
+                copies.append((side_by_side[:, g0 : g0 + 2, :, :], slots.rearrange("p g u r -> p g r u")))
+            return copies
+
+        def copy_out(copies):
+            for target, source in copies:
+                nc.scalar.copy(out=target, in_=source)
 
         def quantize(key):
             kind, i = key
-            values = grouped[key][:].rearrange("p g r u -> p (g r u)").bitcast(BF16)
-            if kind == "x":
-                n, tt = divmod(i, TOK_TILES)
-                cols = slice(tt * P, (tt + 1) * P)
-                for g in range(PASSES):
-                    nc.vector.quantize_mx(
-                        out=x_codes[:, n, g, cols].bitcast(E5M2X4),
-                        scales=x_scales[:, n, g, cols],
-                        in_=values[:, g * 4 * P : (g + 1) * 4 * P],
-                    )
-            else:
+            if kind == "w":
                 codes = work.tile([P, PASSES * P], U32, name="w_codes", tag="w_codes", bufs=10, align_bytes=64)
                 scales = work.tile([P, PASSES * P], U8, name="w_scales", tag="w_scales", bufs=10, align_bytes=64)
+                values = w_grouped[i][:].rearrange("p g r u -> p (g r u)").bitcast(BF16)
                 nc.vector.quantize_mx(out=codes[:].bitcast(E5M2X4), scales=scales[:], in_=values)
                 w_codes[i] = codes
                 w_scales[i] = scales
+            elif i % 2 == 1:
+                b = i // 2
+                cols = slice(b * T, (b + 1) * T)
+                for g in range(PASSES):
+                    values = x_grouped[b][:, g, :, :].rearrange("p r u -> p (r u)").bitcast(BF16)
+                    nc.vector.quantize_mx(out=x_codes[:, g, cols].bitcast(E5M2X4), scales=x_scales[:, g, cols], in_=values)
 
-        def project(j, e, n):
+        def project(j, e, first, count):
             bank = next_bank()
+            tokens = slice(first, first + count)
             for g in range(PASSES):
                 cols = slice(g * P, (g + 1) * P)
                 nc.tensor.matmul_mx(
-                    out=bank[:],
+                    out=bank[:, 0:count],
                     lhsT=w_codes[2 * j + e][:, cols].bitcast(E5M2X4),
                     lhsT_scale=w_scales[2 * j + e][:, cols],
-                    rhs=x_codes[:, n, g, :].bitcast(E5M2X4),
-                    rhs_scale=x_scales[:, n, g, :],
+                    rhs=x_codes[:, g, tokens].bitcast(E5M2X4),
+                    rhs_scale=x_scales[:, g, tokens],
                     start=(g == 0),
                     stop=(g == PASSES - 1),
                 )
             return bank
 
-        def times_table(bank, j, e, which):
-            product = work.tile([P, N_TOK], F32, name="product", tag="product%d%d" % (e, which))
+        def times_table(bank, j, e, which, count):
+            product = work.tile([P, count], F32, name="product", tag="product%d%d" % (e, which), bufs=3)
             nc.vector.scalar_tensor_tensor(
                 out=product[:].rearrange("p (b t) -> p b t", t=T),
-                in0=bank[:].rearrange("p (b t) -> p b t", t=T),
+                in0=bank[:, 0:count].rearrange("p (b t) -> p b t", t=T),
                 scalar=bias[:, 2 * j + e : 2 * j + e + 1],
-                in1=tables[:, which : which + 1, :].to_broadcast([P, N_TOK // T, T]),
+                in1=tables[:, which : which + 1, :].to_broadcast([P, count // T, T]),
                 op0=ALU.add,
                 op1=ALU.mult,
             )
             return product
 
-        def finish(j, n, rotated):
-            gain = gains[:, 0 if j < Q_PAIRS else 1, :].rearrange("p (f i) -> p f i", f=2)
-            result = work.tile([P, TOK_TILES, 2, 2, HALF], F32, name="result", tag="result", bufs=4)
+        def transpose_out(count, rotated):
             banks = []
-            for tt0 in range(0, TOK_TILES, 2):
+            for b in range(count // T):
                 bank = next_bank()
-                slots = bank[:].rearrange("p (t f c) -> p t f c", t=2, f=2)
-                for t in range(2):
+                slots = bank[:].rearrange("p (s f c) -> p s f c", s=2, f=2)
+                for s in range(2):
                     for f in range(2):
-                        cols = slice((tt0 + t) * P, (tt0 + t + 1) * P)
-                        nc.tensor.transpose(slots[:, t, f, :], rotated[f][:, cols], identity[:])
-                banks.append(bank[:].rearrange("p (t f h i) -> p t h f i", t=2, f=2, h=2))
-            scales = []
-            for heads in banks:
-                squares = work.tile([P, 2, 2, 2, HALF], BF16, name="squares", tag="squares", bufs=3)
-                sums = work.tile([P, 4], F32, name="sums", tag="sums", bufs=4)
-                for t in range(2):
+                        cols = slice(b * T + s * P, b * T + (s + 1) * P)
+                        terms = rotated[f]
+                        for n, term in enumerate(terms):
+                            nc.tensor.matmul(
+                                slots[:, s, f, :],
+                                lhsT=term[:, cols],
+                                rhs=identity[:],
+                                is_transpose=True,
+                                start=(n == 0),
+                                stop=(n == len(terms) - 1),
+                            )
+                banks.append(bank[:].rearrange("p (s f h i) -> p s h f i", s=2, f=2, h=2))
+            return banks
+
+        def sum_squares(heads):
+            squares = work.tile([P, 2, 2, 2, HALF], BF16, name="squares", tag="squares", bufs=3)
+            sums = work.tile([P, 4], F32, name="sums", tag="sums", bufs=4)
+            for s in range(2):
+                for h in range(2):
+                    nc.scalar.activation(
+                        out=squares[:, s, h, :, :],
+                        in_=heads[:, s, h, :, :],
+                        func=ACT.Square,
+                        accum_out=sums[:, 2 * s + h : 2 * s + h + 1],
+                    )
+            return sums
+
+        def inverse_root(sums):
+            inverse_rms = work.tile([P, 4], F32, name="inverse_rms", tag="inverse_rms", bufs=4)
+            nc.scalar.activation(out=inverse_rms[:], in_=sums[:], func=ACT.Abs_reciprocal_sqrt, scale=1.0 / HD, bias=EPS)
+            return inverse_rms
+
+        def normalise(j, first, heads, inverse_rms, tiles_on_scalar):
+            gain = gains[:, 0 if j < Q_PAIRS else 1, :]
+            rows, column = (q_rows, j * 2 * HD) if j < Q_PAIRS else (k_rows, (j - Q_PAIRS) * 2 * HD)
+            result = work.tile([P, 2, 2, 2, HALF], F32, name="result", tag="result", bufs=8)
+            if tiles_on_scalar > 0:
+                normed = work.tile([P, tiles_on_scalar, 2, 2, HALF], F32, name="normed", tag="normed", bufs=3)
+                for s in range(tiles_on_scalar):
                     for h in range(2):
                         nc.scalar.activation(
-                            out=squares[:, t, h, :, :],
-                            in_=heads[:, t, h, :, :],
-                            func=ACT.Square,
-                            accum_out=sums[:, 2 * t + h : 2 * t + h + 1],
+                            out=normed[:, s, h, :, :],
+                            in_=heads[:, s, h, :, :],
+                            func=ACT.Copy,
+                            scale=inverse_rms[:, 2 * s + h : 2 * s + h + 1],
                         )
-                inverse_rms = work.tile([P, 4], F32, name="inverse_rms", tag="inverse_rms", bufs=4)
-                nc.scalar.activation(out=inverse_rms[:], in_=sums[:], func=ACT.Abs_reciprocal_sqrt, scale=1.0 / HD, bias=EPS)
-                scales.append(inverse_rms)
-            for half in range(2):
-                for t in range(2):
-                    for h in range(2):
-                        nc.vector.scalar_tensor_tensor(
-                            out=result[:, 2 * half + t, h, :, :],
-                            in0=banks[half][:, t, h, :, :],
-                            scalar=scales[half][:, 2 * t + h : 2 * t + h + 1],
-                            in1=gain,
-                            op0=ALU.mult,
-                            op1=ALU.mult,
-                        )
-            rows, first = (q_rows, j * 2 * HD) if j < Q_PAIRS else (k_rows, (j - Q_PAIRS) * 2 * HD)
-            target = rows[n * N_TOK : (n + 1) * N_TOK, first : first + 2 * HD]
+                nc.gpsimd.tensor_tensor(
+                    out=result[:, 0:tiles_on_scalar, :, :, :].rearrange("p s h f i -> p (s h) (f i)"),
+                    in0=normed[:].rearrange("p s h f i -> p (s h) (f i)"),
+                    in1=gain.unsqueeze(1).to_broadcast([P, 2 * tiles_on_scalar, HD]),
+                    op=ALU.mult,
+                )
+            for s in range(tiles_on_scalar, 2):
+                for h in range(2):
+                    nc.vector.scalar_tensor_tensor(
+                        out=result[:, s, h, :, :],
+                        in0=heads[:, s, h, :, :],
+                        scalar=inverse_rms[:, 2 * s + h : 2 * s + h + 1],
+                        in1=gain.rearrange("p (f i) -> p f i", f=2),
+                        op0=ALU.mult,
+                        op1=ALU.mult,
+                    )
+            target = rows[first : first + T, column : column + 2 * HD]
             nc.sync.dma_start(
-                out=target.rearrange("(t p) c -> p t c", p=P),
-                in_=result[:].rearrange("p t h f i -> p t (h f i)"),
+                out=target.rearrange("(s p) c -> p s c", p=P),
+                in_=result[:].rearrange("p s h f i -> p s (h f i)"),
             )
 
-        for key in order[:RAW_BUFS]:
+        for key in order[:4]:
             load(key)
-        loaded = RAW_BUFS
-
         identity = const.tile([P, P], F32)
         make_identity(nc, identity[:])
 
@@ -193,60 +237,86 @@ def tile_gqaselfattention_pa_kernel(tc, x, Wq, bq, Wk, bk, qn_w, kn_w, cos, sin,
         nc.vector.memset(bias_rows[:], 0.0)
         nc.scalar.dma_start(out=bias_rows[0:Q_PAIRS, :], in_=bq.rearrange("(j c) -> j c", c=2 * P))
         nc.scalar.dma_start(out=bias_rows[Q_PAIRS:PAIRS, :], in_=bk.rearrange("(j c) -> j c", c=2 * P))
+        for key in order[4:RAW_BUFS]:
+            load(key)
+        loaded = RAW_BUFS
         gains = const.tile([P, 2, HD], BF16)
-        nc.scalar.dma_start(out=gains[:, 0, :], in_=qn_w.partition_broadcast(P))
-        nc.scalar.dma_start(out=gains[:, 1, :], in_=kn_w.partition_broadcast(P))
+        nc.sync.dma_start(out=gains[:, 0, :], in_=qn_w.partition_broadcast(P))
+        nc.sync.dma_start(out=gains[:, 1, :], in_=kn_w.partition_broadcast(P))
 
         doubled = const.tile([P, 4, 2, HALF], F32)
         nc.vector.tensor_copy(
             out=doubled[:],
             in_=angles[:].rearrange("p w s i -> p (w s) i").unsqueeze(2).to_broadcast([P, 4, 2, HALF]),
         )
-        tables = const.tile([P, 2, T], F32)
+        tables = const.tile([P, 3, T], F32)
         bias = const.tile([P, 2 * PAIRS], F32)
 
         def transpose_constants():
             bank = next_bank()
             for s in range(4):
                 nc.tensor.transpose(bank[:, s * P : (s + 1) * P], doubled[:, s, :, :].rearrange("p h i -> p (h i)"), identity[:])
-            nc.vector.tensor_copy(out=tables[:].rearrange("p w t -> p (w t)"), in_=bank[:])
+            nc.vector.tensor_copy(out=tables[:, 0:2, :].rearrange("p w t -> p (w t)"), in_=bank[:])
+            nc.vector.tensor_scalar(out=tables[:, 2, :], in0=bank[:, T : 2 * T], scalar1=-1.0, scalar2=None, op0=ALU.mult)
             bank = next_bank()
             nc.tensor.transpose(bank[:, 0:P], bias_rows[:].bitcast(F32), identity[:])
             nc.vector.tensor_copy(out=bias[:], in_=bank[:, 0:PAIRS].bitcast(BF16))
 
         for position, key in enumerate(order[:prologue_tiles]):
-            transpose_in(key)
+            copy_out(transpose_in(key))
             if position == 1:
                 transpose_constants()
-            if position > 0:
-                quantize(order[position - 1])
+            if position < prologue_tiles - 1:
+                quantize(key)
             load(order[loaded])
             loaded += 1
         waiting = [order[prologue_tiles - 1]]
         done = prologue_tiles
 
-        previous = None
-        for k, (j, n) in enumerate(steps):
-            even = project(j, 0, n)
-            odd = project(j, 1, n)
-            even_cos = times_table(even, j, 0, 0)
-            even_sin = times_table(even, j, 0, 1)
+        rotated = []
+        finished = 0
+        first_added_in_psum = len(steps) - 2
+        for k in range(len(steps) + 1):
+            if k < len(steps):
+                j, first, count = steps[k]
+                even = project(j, 0, first, count)
+                odd = project(j, 1, first, count)
+                even_cos = times_table(even, j, 0, 0, count)
+                even_sin = times_table(even, j, 0, 1, count)
+                odd_minus_sin = times_table(odd, j, 1, 2, count)
+                for key in waiting:
+                    quantize(key)
+                odd_cos = times_table(odd, j, 1, 0, count)
+                if k < first_added_in_psum:
+                    first_half = work.tile([P, count], F32, name="first_half", tag="first_half", bufs=LAG + 1)
+                    second_half = work.tile([P, count], F32, name="second_half", tag="second_half", bufs=LAG + 1)
+                    nc.gpsimd.tensor_tensor(out=first_half[:], in0=even_cos[:], in1=odd_minus_sin[:], op=ALU.add)
+                    nc.gpsimd.tensor_tensor(out=second_half[:], in0=even_sin[:], in1=odd_cos[:], op=ALU.add)
+                    rotated.append(([first_half], [second_half]))
+                else:
+                    rotated.append(([even_cos, odd_minus_sin], [even_sin, odd_cos]))
+                waiting = order[done : done + tiles_in_step[k]]
+                done += tiles_in_step[k]
+            else:
+                waiting = []
+            ready = []
+            while finished <= k - (LAG if k <= first_added_in_psum else 1):
+                j, first, count = steps[finished]
+                for b, heads in enumerate(transpose_out(count, rotated[finished])):
+                    ready.append((j, first + b * T, heads))
+                finished += 1
+            sums = [sum_squares(heads) for j, first, heads in ready]
+            copies = transpose_in(waiting[0]) if waiting else []
+            roots = []
+            for b in range(len(ready)):
+                roots.append(inverse_root(sums[b]))
+                copy_out(copies[b : b + 1])
+            copy_out(copies[len(ready) :])
+            for b, (j, first, heads) in enumerate(ready):
+                normalise(j, first, heads, roots[b], TILES_ON_SCALAR if b % 2 == 1 and k < len(steps) + 1 - 2 else 0)
+            for key in waiting[1:]:
+                copy_out(transpose_in(key))
             for key in waiting:
-                quantize(key)
-            odd_sin = times_table(odd, j, 1, 1)
-            odd_cos = times_table(odd, j, 1, 0)
-            first_half = work.tile([P, N_TOK], F32, name="first_half", tag="first_half")
-            second_half = work.tile([P, N_TOK], F32, name="second_half", tag="second_half")
-            nc.gpsimd.tensor_tensor(out=first_half[:], in0=even_cos[:], in1=odd_sin[:], op=ALU.subtract)
-            nc.gpsimd.tensor_tensor(out=second_half[:], in0=even_sin[:], in1=odd_cos[:], op=ALU.add)
-            if previous is not None:
-                finish(*previous)
-            previous = (j, n, (first_half, second_half))
-            waiting = order[done : done + tiles_in_step[k]]
-            done += tiles_in_step[k]
-            for key in waiting:
-                transpose_in(key)
                 if loaded < len(order):
                     load(order[loaded])
                     loaded += 1
-        finish(*previous)

@@ -24,9 +24,7 @@ PAIRS = (HQ + HKV) // 2
 BANKS = 8
 BANK_COLS = 512
 RAW_BUFS = 12
-EARLY_PAIRS = 3
 LAG = 2
-TILES_ON_SCALAR = 2
 
 
 def tile_gqaselfattention_pa_kernel(tc, x, Wq, bq, Wk, bk, qn_w, kn_w, cos, sin, out_0, out_1):
@@ -35,15 +33,14 @@ def tile_gqaselfattention_pa_kernel(tc, x, Wq, bq, Wk, bk, qn_w, kn_w, cos, sin,
     q_rows = out_0.rearrange("b t h d -> (b t) (h d)")
     k_rows = out_1.rearrange("b t h d -> (b t) (h d)")
 
-    steps = [(0, 0, T), (0, T, T)] + [(j, 0, N_TOK) for j in range(1, EARLY_PAIRS)]
-    steps += [(j, N_TOK, N_TOK) for j in range(EARLY_PAIRS)]
-    steps += [(j, first, N_TOK) for j in range(EARLY_PAIRS, PAIRS) for first in (0, N_TOK)]
+    steps = [(0, b * T, T) for b in range(B)]
+    steps += [(j, first, N_TOK) for j in range(1, PAIRS) for first in (0, N_TOK)]
     steps = steps[:-1] + [(PAIRS - 1, N_TOK, T), (PAIRS - 1, N_TOK + T, T)]
     x_tiles = [("x", i) for i in range(2 * B)]
     w_tiles = [("w", i) for i in range(2 * PAIRS)]
-    order = x_tiles[:2] + w_tiles[:2] + x_tiles[2:4] + w_tiles[2 : 2 * EARLY_PAIRS] + x_tiles[4:] + w_tiles[2 * EARLY_PAIRS :]
+    order = x_tiles[:2] + w_tiles[:2] + x_tiles[2:] + w_tiles[2:]
     prologue_tiles = 6
-    tiles_in_step = [2, 2, 4] + [1] * (2 * (PAIRS - EARLY_PAIRS))
+    tiles_in_step = [2, 2, 2] + [1] * (2 * (PAIRS - 2))
     tiles_in_step += [0] * (len(steps) - len(tiles_in_step))
 
     with ExitStack() as ctx:
@@ -77,12 +74,15 @@ def tile_gqaselfattention_pa_kernel(tc, x, Wq, bq, Wk, bk, qn_w, kn_w, cos, sin,
                 j, e = divmod(i, 2)
                 weight, first = (Wq, j * 2 * P) if j < Q_PAIRS else (Wk, (j - Q_PAIRS) * 2 * P)
                 source = weight[first : first + 2 * P, :].rearrange("(p e) c -> p e c", e=2)[:, e, :]
-            nc.sync.dma_start(out=rows[:], in_=source)
+            pieces = 2 if key == order[0] else 1
+            for n in range(pieces):
+                cols = slice(n * C // pieces, (n + 1) * C // pieces)
+                nc.sync.dma_start(out=rows[:, cols], in_=source[:, cols])
             raw[key] = rows
 
         def transpose_in(key):
             kind, i = key
-            words = raw[key][:].bitcast(F32)
+            words = raw[key][:].bitcast(F32).rearrange("p (g r u) -> p g u r", g=PASSES, u=2)
             if kind == "w":
                 w_grouped[i] = work.tile([P, PASSES, P, 2], F32, name="w_grouped", tag="w_grouped", bufs=3, align_bytes=64)
                 side_by_side = w_grouped[i][:]
@@ -97,8 +97,7 @@ def tile_gqaselfattention_pa_kernel(tc, x, Wq, bq, Wk, bk, qn_w, kn_w, cos, sin,
                 slots = bank[:].rearrange("p (g u r) -> p g u r", g=2, u=2)
                 for g in range(2):
                     for u in range(2):
-                        first = 2 * P * (g0 + g)
-                        nc.tensor.transpose(slots[:, g, u, :], words[:, first + u : first + 2 * P : 2], identity[:])
+                        nc.tensor.transpose(slots[:, g, u, :], words[:, g0 + g, u, :], identity[:])
                 copies.append((side_by_side[:, g0 : g0 + 2, :, :], slots.rearrange("p g u r -> p g r u")))
             return copies
 
@@ -138,38 +137,34 @@ def tile_gqaselfattention_pa_kernel(tc, x, Wq, bq, Wk, bk, qn_w, kn_w, cos, sin,
                 )
             return bank
 
-        def times_table(bank, j, e, which, count):
-            product = work.tile([P, count], F32, name="product", tag="product%d%d" % (e, which), bufs=3)
+        def times_tables(bank, j, e, count):
+            products = work.tile([P, 2, count], F32, name="products", tag="products%d" % e, bufs=3)
             nc.vector.scalar_tensor_tensor(
-                out=product[:].rearrange("p (b t) -> p b t", t=T),
-                in0=bank[:, 0:count].rearrange("p (b t) -> p b t", t=T),
+                out=products[:],
+                in0=bank[:, 0:count].unsqueeze(1).to_broadcast([P, 2, count]),
                 scalar=bias[:, 2 * j + e : 2 * j + e + 1],
-                in1=tables[:, which : which + 1, :].to_broadcast([P, count // T, T]),
+                in1=tables[:, 1 - e : 3 - e, 0:count],
                 op0=ALU.add,
                 op1=ALU.mult,
             )
-            return product
+            return products
 
-        def transpose_out(count, rotated):
-            banks = []
-            for b in range(count // T):
-                bank = next_bank()
-                slots = bank[:].rearrange("p (s f c) -> p s f c", s=2, f=2)
-                for s in range(2):
-                    for f in range(2):
-                        cols = slice(b * T + s * P, b * T + (s + 1) * P)
-                        terms = rotated[f]
-                        for n, term in enumerate(terms):
-                            nc.tensor.matmul(
-                                slots[:, s, f, :],
-                                lhsT=term[:, cols],
-                                rhs=identity[:],
-                                is_transpose=True,
-                                start=(n == 0),
-                                stop=(n == len(terms) - 1),
-                            )
-                banks.append(bank[:].rearrange("p (s f h i) -> p s h f i", s=2, f=2, h=2))
-            return banks
+        def transpose_out(terms, b):
+            bank = next_bank()
+            slots = bank[:].rearrange("p (s f c) -> p s f c", s=2, f=2)
+            for s in range(2):
+                cols = slice(b * T + s * P, b * T + (s + 1) * P)
+                for f in range(2):
+                    for n, term in enumerate(terms):
+                        nc.tensor.matmul(
+                            slots[:, s, f, :],
+                            lhsT=term[:, f, cols],
+                            rhs=identity[:],
+                            is_transpose=True,
+                            start=(n == 0),
+                            stop=(n == len(terms) - 1),
+                        )
+            return bank[:].rearrange("p (s f h i) -> p s h f i", s=2, f=2, h=2)
 
         def sum_squares(heads):
             squares = work.tile([P, 2, 2, 2, HALF], BF16, name="squares", tag="squares", bufs=3)
@@ -189,43 +184,41 @@ def tile_gqaselfattention_pa_kernel(tc, x, Wq, bq, Wk, bk, qn_w, kn_w, cos, sin,
             nc.scalar.activation(out=inverse_rms[:], in_=sums[:], func=ACT.Abs_reciprocal_sqrt, scale=1.0 / HD, bias=EPS)
             return inverse_rms
 
-        def normalise(j, first, heads, inverse_rms, tiles_on_scalar):
+        def normalise(j, first, heads, inverse_rms, heads_on_scalar):
             gain = gains[:, 0 if j < Q_PAIRS else 1, :]
             rows, column = (q_rows, j * 2 * HD) if j < Q_PAIRS else (k_rows, (j - Q_PAIRS) * 2 * HD)
-            result = work.tile([P, 2, 2, 2, HALF], F32, name="result", tag="result", bufs=8)
-            if tiles_on_scalar > 0:
-                normed = work.tile([P, tiles_on_scalar, 2, 2, HALF], F32, name="normed", tag="normed", bufs=3)
-                for s in range(tiles_on_scalar):
-                    for h in range(2):
-                        nc.scalar.activation(
-                            out=normed[:, s, h, :, :],
-                            in_=heads[:, s, h, :, :],
-                            func=ACT.Copy,
-                            scale=inverse_rms[:, 2 * s + h : 2 * s + h + 1],
-                        )
+            result = work.tile([P, 4, 2, HALF], F32, name="result", tag="result", bufs=8)
+            for n in range(heads_on_scalar, 4):
+                nc.vector.scalar_tensor_tensor(
+                    out=result[:, n, :, :],
+                    in0=heads[:, n // 2, n % 2, :, :],
+                    scalar=inverse_rms[:, n : n + 1],
+                    in1=gain.rearrange("p (f i) -> p f i", f=2),
+                    op0=ALU.mult,
+                    op1=ALU.mult,
+                )
+            if heads_on_scalar > 0:
+                normed = work.tile([P, heads_on_scalar, 2, HALF], F32, name="normed", tag="normed", bufs=3)
+                for n in range(heads_on_scalar):
+                    nc.scalar.activation(
+                        out=normed[:, n, :, :],
+                        in_=heads[:, n // 2, n % 2, :, :],
+                        func=ACT.Copy,
+                        scale=inverse_rms[:, n : n + 1],
+                    )
                 nc.gpsimd.tensor_tensor(
-                    out=result[:, 0:tiles_on_scalar, :, :, :].rearrange("p s h f i -> p (s h) (f i)"),
-                    in0=normed[:].rearrange("p s h f i -> p (s h) (f i)"),
-                    in1=gain.unsqueeze(1).to_broadcast([P, 2 * tiles_on_scalar, HD]),
+                    out=result[:, 0:heads_on_scalar, :, :].rearrange("p n f i -> p n (f i)"),
+                    in0=normed[:].rearrange("p n f i -> p n (f i)"),
+                    in1=wide_gains[:, 0 if j < Q_PAIRS else 1, 0:heads_on_scalar, :],
                     op=ALU.mult,
                 )
-            for s in range(tiles_on_scalar, 2):
-                for h in range(2):
-                    nc.vector.scalar_tensor_tensor(
-                        out=result[:, s, h, :, :],
-                        in0=heads[:, s, h, :, :],
-                        scalar=inverse_rms[:, 2 * s + h : 2 * s + h + 1],
-                        in1=gain.rearrange("p (f i) -> p f i", f=2),
-                        op0=ALU.mult,
-                        op1=ALU.mult,
-                    )
             target = rows[first : first + T, column : column + 2 * HD]
             nc.sync.dma_start(
                 out=target.rearrange("(s p) c -> p s c", p=P),
-                in_=result[:].rearrange("p s h f i -> p s (h f i)"),
+                in_=result[:].rearrange("p (s h) f i -> p s (h f i)", s=2),
             )
 
-        for key in order[:4]:
+        for key in order[:3]:
             load(key)
         identity = const.tile([P, P], F32)
         make_identity(nc, identity[:])
@@ -237,27 +230,30 @@ def tile_gqaselfattention_pa_kernel(tc, x, Wq, bq, Wk, bk, qn_w, kn_w, cos, sin,
         nc.vector.memset(bias_rows[:], 0.0)
         nc.scalar.dma_start(out=bias_rows[0:Q_PAIRS, :], in_=bq.rearrange("(j c) -> j c", c=2 * P))
         nc.scalar.dma_start(out=bias_rows[Q_PAIRS:PAIRS, :], in_=bk.rearrange("(j c) -> j c", c=2 * P))
-        for key in order[4:RAW_BUFS]:
+        for key in order[3:RAW_BUFS]:
             load(key)
         loaded = RAW_BUFS
         gains = const.tile([P, 2, HD], BF16)
         nc.sync.dma_start(out=gains[:, 0, :], in_=qn_w.partition_broadcast(P))
         nc.sync.dma_start(out=gains[:, 1, :], in_=kn_w.partition_broadcast(P))
 
+        wide_gains = const.tile([P, 2, 4, HD], F32)
         doubled = const.tile([P, 4, 2, HALF], F32)
         nc.vector.tensor_copy(
             out=doubled[:],
             in_=angles[:].rearrange("p w s i -> p (w s) i").unsqueeze(2).to_broadcast([P, 4, 2, HALF]),
         )
-        tables = const.tile([P, 3, T], F32)
+        tables = const.tile([P, 3, N_TOK], F32)
         bias = const.tile([P, 2 * PAIRS], F32)
 
         def transpose_constants():
             bank = next_bank()
             for s in range(4):
                 nc.tensor.transpose(bank[:, s * P : (s + 1) * P], doubled[:, s, :, :].rearrange("p h i -> p (h i)"), identity[:])
-            nc.vector.tensor_copy(out=tables[:, 0:2, :].rearrange("p w t -> p (w t)"), in_=bank[:])
-            nc.vector.tensor_scalar(out=tables[:, 2, :], in0=bank[:, T : 2 * T], scalar1=-1.0, scalar2=None, op0=ALU.mult)
+            repeated = bank[:].rearrange("p (w t) -> p w t", w=2).unsqueeze(2).to_broadcast([P, 2, N_TOK // T, T])
+            per_batch = tables[:].rearrange("p w (b t) -> p w b t", t=T)
+            nc.vector.tensor_copy(out=per_batch[:, 1:3, :, :], in_=repeated)
+            nc.vector.tensor_scalar(out=per_batch[:, 0, :, :], in0=repeated[:, 1, :, :], scalar1=-1.0, scalar2=None, op0=ALU.mult)
             bank = next_bank()
             nc.tensor.transpose(bank[:, 0:P], bias_rows[:].bitcast(F32), identity[:])
             nc.vector.tensor_copy(out=bias[:], in_=bank[:, 0:PAIRS].bitcast(BF16))
@@ -274,49 +270,56 @@ def tile_gqaselfattention_pa_kernel(tc, x, Wq, bq, Wk, bk, qn_w, kn_w, cos, sin,
         done = prologue_tiles
 
         rotated = []
+        units = [(step, b) for step, (j, first, count) in enumerate(steps) for b in range(count // T)]
         finished = 0
-        first_added_in_psum = len(steps) - 2
+        first_added_in_psum = len(steps) - 4
         for k in range(len(steps) + 1):
             if k < len(steps):
                 j, first, count = steps[k]
                 even = project(j, 0, first, count)
                 odd = project(j, 1, first, count)
-                even_cos = times_table(even, j, 0, 0, count)
-                even_sin = times_table(even, j, 0, 1, count)
-                odd_minus_sin = times_table(odd, j, 1, 2, count)
+                even_products = times_tables(even, j, 0, count)
+                odd_products = times_tables(odd, j, 1, count)
                 for key in waiting:
                     quantize(key)
-                odd_cos = times_table(odd, j, 1, 0, count)
-                if k < first_added_in_psum:
-                    first_half = work.tile([P, count], F32, name="first_half", tag="first_half", bufs=LAG + 1)
-                    second_half = work.tile([P, count], F32, name="second_half", tag="second_half", bufs=LAG + 1)
-                    nc.gpsimd.tensor_tensor(out=first_half[:], in0=even_cos[:], in1=odd_minus_sin[:], op=ALU.add)
-                    nc.gpsimd.tensor_tensor(out=second_half[:], in0=even_sin[:], in1=odd_cos[:], op=ALU.add)
-                    rotated.append(([first_half], [second_half]))
-                else:
-                    rotated.append(([even_cos, odd_minus_sin], [even_sin, odd_cos]))
+                if k == B - 1:
+                    nc.vector.tensor_copy(out=wide_gains[:], in_=gains[:].unsqueeze(2).to_broadcast([P, 2, 4, HD]))
                 waiting = order[done : done + tiles_in_step[k]]
                 done += tiles_in_step[k]
+                if k < first_added_in_psum:
+                    halves = work.tile([P, 2, count], F32, name="halves", tag="halves", bufs=LAG + 1)
+                    nc.gpsimd.tensor_tensor(out=halves[:], in0=even_products[:], in1=odd_products[:], op=ALU.add)
+                    rotated.append([halves])
+                else:
+                    rotated.append([even_products, odd_products])
             else:
                 waiting = []
+            catching_up = k >= len(steps) - 4
+            lag = 1 if catching_up else LAG
+            due = [unit for unit in units[finished : finished + 3] if unit[0] <= k - lag]
             ready = []
-            while finished <= k - (LAG if k <= first_added_in_psum else 1):
-                j, first, count = steps[finished]
-                for b, heads in enumerate(transpose_out(count, rotated[finished])):
-                    ready.append((j, first + b * T, heads))
-                finished += 1
-            sums = [sum_squares(heads) for j, first, heads in ready]
+            for step, b in due:
+                j, first, count = steps[step]
+                ready.append((j, first + b * T, transpose_out(rotated[step], b)))
             copies = transpose_in(waiting[0]) if waiting else []
+            sums = [sum_squares(heads) for j, first, heads in ready[:2]]
             roots = []
             for b in range(len(ready)):
                 roots.append(inverse_root(sums[b]))
                 copy_out(copies[b : b + 1])
+                if b + 2 < len(ready):
+                    sums.append(sum_squares(ready[b + 2][2]))
             copy_out(copies[len(ready) :])
             for b, (j, first, heads) in enumerate(ready):
-                normalise(j, first, heads, roots[b], TILES_ON_SCALAR if b % 2 == 1 and k < len(steps) + 1 - 2 else 0)
+                on_scalar = 4 if catching_up else 3
+                if b != 1 or finished + b >= len(units) - 1:
+                    on_scalar = 0
+                normalise(j, first, heads, roots[b], on_scalar)
+            finished += len(due)
             for key in waiting[1:]:
                 copy_out(transpose_in(key))
             for key in waiting:
                 if loaded < len(order):
                     load(order[loaded])
                     loaded += 1
+        assert finished == len(units)

@@ -184,7 +184,7 @@ def tile_gqaselfattention_pa_kernel(tc, x, Wq, bq, Wk, bk, qn_w, kn_w, cos, sin,
             nc.scalar.activation(out=inverse_rms[:], in_=sums[:], func=ACT.Abs_reciprocal_sqrt, scale=1.0 / HD, bias=EPS)
             return inverse_rms
 
-        def normalise(j, first, heads, inverse_rms, heads_on_scalar):
+        def normalise(j, first, heads, inverse_rms, heads_on_scalar, is_last):
             gain = gains[:, 0 if j < Q_PAIRS else 1, :]
             rows, column = (q_rows, j * 2 * HD) if j < Q_PAIRS else (k_rows, (j - Q_PAIRS) * 2 * HD)
             result = work.tile([P, 4, 2, HALF], F32, name="result", tag="result", bufs=8)
@@ -212,11 +212,13 @@ def tile_gqaselfattention_pa_kernel(tc, x, Wq, bq, Wk, bk, qn_w, kn_w, cos, sin,
                     in1=wide_gains[:, 0 if j < Q_PAIRS else 1, 0:heads_on_scalar, :],
                     op=ALU.mult,
                 )
-            target = rows[first : first + T, column : column + 2 * HD]
-            nc.sync.dma_start(
-                out=target.rearrange("(s p) c -> p s c", p=P),
-                in_=result[:].rearrange("p (s h) f i -> p s (h f i)", s=2),
-            )
+            target = rows[first : first + T, column : column + 2 * HD].rearrange("(s p) c -> p s c", p=P)
+            source = result[:].rearrange("p (s h) f i -> p s (h f i)", s=2)
+            if is_last:
+                for s in range(2):
+                    nc.sync.dma_start(out=target[:, s, :], in_=source[:, s, :])
+            else:
+                nc.sync.dma_start(out=target, in_=source)
 
         for key in order[:3]:
             load(key)
@@ -272,6 +274,7 @@ def tile_gqaselfattention_pa_kernel(tc, x, Wq, bq, Wk, bk, qn_w, kn_w, cos, sin,
         rotated = []
         units = [(step, b) for step, (j, first, count) in enumerate(steps) for b in range(count // T)]
         finished = 0
+        deferred = []
         first_added_in_psum = len(steps) - 4
         for k in range(len(steps) + 1):
             if k < len(steps):
@@ -294,6 +297,9 @@ def tile_gqaselfattention_pa_kernel(tc, x, Wq, bq, Wk, bk, qn_w, kn_w, cos, sin,
                     rotated.append([even_products, odd_products])
             else:
                 waiting = []
+            for job in deferred:
+                normalise(*job)
+            deferred = []
             catching_up = k >= len(steps) - 4
             lag = 1 if catching_up else LAG
             due = [unit for unit in units[finished : finished + 3] if unit[0] <= k - lag]
@@ -312,9 +318,12 @@ def tile_gqaselfattention_pa_kernel(tc, x, Wq, bq, Wk, bk, qn_w, kn_w, cos, sin,
             copy_out(copies[len(ready) :])
             for b, (j, first, heads) in enumerate(ready):
                 on_scalar = 4 if catching_up else 3
-                if b != 1 or finished + b >= len(units) - 1:
+                if b != 1 or finished + b >= len(units) - 4:
                     on_scalar = 0
-                normalise(j, first, heads, roots[b], on_scalar)
+                if k >= len(steps) - 3:
+                    deferred.append((j, first, heads, roots[b], on_scalar, finished + b == len(units) - 1))
+                else:
+                    normalise(j, first, heads, roots[b], on_scalar, False)
             finished += len(due)
             for key in waiting[1:]:
                 copy_out(transpose_in(key))
@@ -322,4 +331,6 @@ def tile_gqaselfattention_pa_kernel(tc, x, Wq, bq, Wk, bk, qn_w, kn_w, cos, sin,
                 if loaded < len(order):
                     load(order[loaded])
                     loaded += 1
+        for job in deferred:
+            normalise(*job)
         assert finished == len(units)

@@ -232,6 +232,8 @@ def tile_gqaselfattention_pa_kernel(tc, x, Wq, bq, Wk, bk, qn_w, kn_w, cos, sin,
         nc.vector.memset(bias_rows[:], 0.0)
         nc.scalar.dma_start(out=bias_rows[0:Q_PAIRS, :], in_=bq.rearrange("(j c) -> j c", c=2 * P))
         nc.scalar.dma_start(out=bias_rows[Q_PAIRS:PAIRS, :], in_=bk.rearrange("(j c) -> j c", c=2 * P))
+        unread = const.tile([P, 1], F32)
+        nc.scalar.activation(out=unread[:], in_=identity[:, 0:1], func=ACT.Abs_reciprocal_sqrt, scale=1.0 / HD, bias=EPS)
         for key in order[3:RAW_BUFS]:
             load(key)
         loaded = RAW_BUFS

from contextlib import ExitStack

import concourse.mybir as mybir
from concourse.masks import make_identity

F32 = mybir.dt.float32
BF16 = mybir.dt.bfloat16
U32 = mybir.dt.uint32
U8 = mybir.dt.uint8
E5M2X4 = mybir.dt.float8_e5m2_x4
ALU = mybir.AluOpType
ACT = mybir.ActivationFunctionType

B, T, C, HQ, HKV, HD = 4, 256, 2048, 16, 4, 128
EPS = 1e-6
FLOPS = 2 * B * T * C * (HQ + HKV) * HD

P = 128
HALF = HD // 2
PASSES = C // 512
N_TOK = 512
Q_PAIRS = HQ // 2
PAIRS = (HQ + HKV) // 2
BANKS = 8
BANK_COLS = 512
RAW_BUFS = 12
LAG = 2


def tile_gqaselfattention_pa_kernel(tc, x, Wq, bq, Wk, bk, qn_w, kn_w, cos, sin, out_0, out_1):
    nc = tc.nc
    x_rows = x.rearrange("b t c -> (b t) c")
    q_rows = out_0.rearrange("b t h d -> (b t) (h d)")
    k_rows = out_1.rearrange("b t h d -> (b t) (h d)")

    steps = [(0, b * T, T) for b in range(B)]
    steps += [(j, first, N_TOK) for j in range(1, PAIRS) for first in (0, N_TOK)]
    steps = steps[:-1] + [(PAIRS - 1, N_TOK, T), (PAIRS - 1, N_TOK + T, T)]
    x_tiles = [("x", i) for i in range(2 * B)]
    w_tiles = [("w", i) for i in range(2 * PAIRS)]
    order = x_tiles[:2] + w_tiles[:2] + x_tiles[2:] + w_tiles[2:]
    prologue_tiles = 6
    tiles_in_step = [2, 2, 2] + [1] * (2 * (PAIRS - 2))
    tiles_in_step += [0] * (len(steps) - len(tiles_in_step))

    with ExitStack() as ctx:
        const = ctx.enter_context(tc.tile_pool(name="const", bufs=1))
        raw_pool = ctx.enter_context(tc.tile_pool(name="raw", bufs=RAW_BUFS))
        work = ctx.enter_context(tc.tile_pool(name="work", bufs=2))
        psum = ctx.enter_context(tc.psum_pool(name="psum", bufs=1))
        ctx.enter_context(tc.manual_schedule())

        banks_taken = []

        def next_bank():
            index = len(banks_taken) % BANKS
            banks_taken.append(index)
            return psum.tile([P, BANK_COLS], F32, name="bank%d" % index, tag="bank%d" % index)

        raw = {}
        x_grouped = {}
        w_grouped = {}
        x_codes = const.tile([P, PASSES, B * T], U32, align_bytes=64)
        x_scales = const.tile([P, PASSES, B * T], U8, align_bytes=64)
        w_codes = {}
        w_scales = {}

        def load(key):
            kind, i = key
            rows = raw_pool.tile([P, C], BF16, name="rows", tag="rows")
            if kind == "x":
                source = x_rows[i * P : (i + 1) * P, :]
            else:
                j, e = divmod(i, 2)
                weight, first = (Wq, j * 2 * P) if j < Q_PAIRS else (Wk, (j - Q_PAIRS) * 2 * P)
                source = weight[first : first + 2 * P, :].rearrange("(p e) c -> p e c", e=2)[:, e, :]
            pieces = 2 if key == order[0] else 1
            for n in range(pieces):
                cols = slice(n * C // pieces, (n + 1) * C // pieces)
                nc.sync.dma_start(out=rows[:, cols], in_=source[:, cols])
            raw[key] = rows

        def transpose_in(key):
            kind, i = key
            words = raw[key][:].bitcast(F32).rearrange("p (g r u) -> p g u r", g=PASSES, u=2)
            if kind == "w":
                w_grouped[i] = work.tile([P, PASSES, P, 2], F32, name="w_grouped", tag="w_grouped", bufs=3, align_bytes=64)
                side_by_side = w_grouped[i][:]
            else:
                b, s = divmod(i, 2)
                if s == 0:
                    x_grouped[b] = work.tile([P, PASSES, T, 2], F32, name="x_grouped", tag="x_grouped", align_bytes=64)
                side_by_side = x_grouped[b][:, :, s * P : (s + 1) * P, :]
            copies = []
            for g0 in range(0, PASSES, 2):
                bank = next_bank()
                slots = bank[:].rearrange("p (g u r) -> p g u r", g=2, u=2)
                for g in range(2):
                    for u in range(2):
                        nc.tensor.transpose(slots[:, g, u, :], words[:, g0 + g, u, :], identity[:])
                copies.append((side_by_side[:, g0 : g0 + 2, :, :], slots.rearrange("p g u r -> p g r u")))
            return copies

        def copy_out(copies):
            for target, source in copies:
                nc.scalar.copy(out=target, in_=source)

        def quantize(key):
            kind, i = key
            if kind == "w":
                codes = work.tile([P, PASSES * P], U32, name="w_codes", tag="w_codes", bufs=10, align_bytes=64)
                scales = work.tile([P, PASSES * P], U8, name="w_scales", tag="w_scales", bufs=10, align_bytes=64)
                values = w_grouped[i][:].rearrange("p g r u -> p (g r u)").bitcast(BF16)
                nc.vector.quantize_mx(out=codes[:].bitcast(E5M2X4), scales=scales[:], in_=values)
                w_codes[i] = codes
                w_scales[i] = scales
            elif i % 2 == 1:
                b = i // 2
                cols = slice(b * T, (b + 1) * T)
                for g in range(PASSES):
                    values = x_grouped[b][:, g, :, :].rearrange("p r u -> p (r u)").bitcast(BF16)
                    nc.vector.quantize_mx(out=x_codes[:, g, cols].bitcast(E5M2X4), scales=x_scales[:, g, cols], in_=values)

        def project(j, e, first, count):
            bank = next_bank()
            tokens = slice(first, first + count)
            for g in range(PASSES):
                cols = slice(g * P, (g + 1) * P)
                nc.tensor.matmul_mx(
                    out=bank[:, 0:count],
                    lhsT=w_codes[2 * j + e][:, cols].bitcast(E5M2X4),
                    lhsT_scale=w_scales[2 * j + e][:, cols],
                    rhs=x_codes[:, g, tokens].bitcast(E5M2X4),
                    rhs_scale=x_scales[:, g, tokens],
                    start=(g == 0),
                    stop=(g == PASSES - 1),
                )
            return bank

        def times_tables(bank, j, e, count):
            products = work.tile([P, 2, count], F32, name="products", tag="products%d" % e, bufs=3)
            nc.vector.scalar_tensor_tensor(
                out=products[:],
                in0=bank[:, 0:count].unsqueeze(1).to_broadcast([P, 2, count]),
                scalar=bias[:, 2 * j + e : 2 * j + e + 1],
                in1=tables[:, 1 - e : 3 - e, 0:count],
                op0=ALU.add,
                op1=ALU.mult,
            )
            return products

        def transpose_out(terms, b):
            bank = next_bank()
            slots = bank[:].rearrange("p (s f c) -> p s f c", s=2, f=2)
            for s in range(2):
                cols = slice(b * T + s * P, b * T + (s + 1) * P)
                for f in range(2):
                    for n, term in enumerate(terms):
                        nc.tensor.matmul(
                            slots[:, s, f, :],
                            lhsT=term[:, f, cols],
                            rhs=identity[:],
                            is_transpose=True,
                            start=(n == 0),
                            stop=(n == len(terms) - 1),
                        )
            return bank[:].rearrange("p (s f h i) -> p s h f i", s=2, f=2, h=2)

        def sum_squares(heads):
            squares = work.tile([P, 2, 2, 2, HALF], BF16, name="squares", tag="squares", bufs=3)
            sums = work.tile([P, 4], F32, name="sums", tag="sums", bufs=4)
            for s in range(2):
                for h in range(2):
                    nc.scalar.activation(
                        out=squares[:, s, h, :, :],
                        in_=heads[:, s, h, :, :],
                        func=ACT.Square,
                        accum_out=sums[:, 2 * s + h : 2 * s + h + 1],
                    )
            return sums

        def inverse_root(sums):
            inverse_rms = work.tile([P, 4], F32, name="inverse_rms", tag="inverse_rms", bufs=4)
            nc.scalar.activation(out=inverse_rms[:], in_=sums[:], func=ACT.Abs_reciprocal_sqrt, scale=1.0 / HD, bias=EPS)
            return inverse_rms

        def normalise(j, first, heads, inverse_rms, heads_on_scalar, is_last):
            gain = gains[:, 0 if j < Q_PAIRS else 1, :]
            rows, column = (q_rows, j * 2 * HD) if j < Q_PAIRS else (k_rows, (j - Q_PAIRS) * 2 * HD)
            result = work.tile([P, 4, 2, HALF], F32, name="result", tag="result", bufs=8)
            for n in range(heads_on_scalar, 4):
                nc.vector.scalar_tensor_tensor(
                    out=result[:, n, :, :],
                    in0=heads[:, n // 2, n % 2, :, :],
                    scalar=inverse_rms[:, n : n + 1],
                    in1=gain.rearrange("p (f i) -> p f i", f=2),
                    op0=ALU.mult,
                    op1=ALU.mult,
                )
            if heads_on_scalar > 0:
                normed = work.tile([P, heads_on_scalar, 2, HALF], F32, name="normed", tag="normed", bufs=3)
                for n in range(heads_on_scalar):
                    nc.scalar.activation(
                        out=normed[:, n, :, :],
                        in_=heads[:, n // 2, n % 2, :, :],
                        func=ACT.Copy,
                        scale=inverse_rms[:, n : n + 1],
                    )
                nc.gpsimd.tensor_tensor(
                    out=result[:, 0:heads_on_scalar, :, :].rearrange("p n f i -> p n (f i)"),
                    in0=normed[:].rearrange("p n f i -> p n (f i)"),
                    in1=wide_gains[:, 0 if j < Q_PAIRS else 1, 0:heads_on_scalar, :],
                    op=ALU.mult,
                )
            target = rows[first : first + T, column : column + 2 * HD].rearrange("(s p) c -> p s c", p=P)
            source = result[:].rearrange("p (s h) f i -> p s (h f i)", s=2)
            if is_last:
                for s in range(2):
                    nc.sync.dma_start(out=target[:, s, :], in_=source[:, s, :])
            else:
                nc.sync.dma_start(out=target, in_=source)

        for key in order[:3]:
            load(key)
        identity = const.tile([P, P], F32)
        make_identity(nc, identity[:])

        angles = const.tile([P, 2, 2, HALF], BF16)
        nc.scalar.dma_start(out=angles[:, 0, :, :], in_=cos.rearrange("(s p) i -> p s i", p=P))
        nc.scalar.dma_start(out=angles[:, 1, :, :], in_=sin.rearrange("(s p) i -> p s i", p=P))
        bias_rows = const.tile([P, 2 * P], BF16)
        nc.vector.memset(bias_rows[:], 0.0)
        nc.scalar.dma_start(out=bias_rows[0:Q_PAIRS, :], in_=bq.rearrange("(j c) -> j c", c=2 * P))
        nc.scalar.dma_start(out=bias_rows[Q_PAIRS:PAIRS, :], in_=bk.rearrange("(j c) -> j c", c=2 * P))
        unread = const.tile([P, 1], F32)
        nc.scalar.activation(out=unread[:], in_=identity[:, 0:1], func=ACT.Abs_reciprocal_sqrt, scale=1.0 / HD, bias=EPS)
        for key in order[3:RAW_BUFS]:
            load(key)
        loaded = RAW_BUFS
        gains = const.tile([P, 2, HD], BF16)
        nc.sync.dma_start(out=gains[:, 0, :], in_=qn_w.partition_broadcast(P))
        nc.sync.dma_start(out=gains[:, 1, :], in_=kn_w.partition_broadcast(P))

        wide_gains = const.tile([P, 2, 4, HD], F32)
        doubled = const.tile([P, 4, 2, HALF], F32)
        nc.vector.tensor_copy(
            out=doubled[:],
            in_=angles[:].rearrange("p w s i -> p (w s) i").unsqueeze(2).to_broadcast([P, 4, 2, HALF]),
        )
        tables = const.tile([P, 3, N_TOK], F32)
        bias = const.tile([P, 2 * PAIRS], F32)

        def transpose_constants():
            bank = next_bank()
            for s in range(4):
                nc.tensor.transpose(bank[:, s * P : (s + 1) * P], doubled[:, s, :, :].rearrange("p h i -> p (h i)"), identity[:])
            repeated = bank[:].rearrange("p (w t) -> p w t", w=2).unsqueeze(2).to_broadcast([P, 2, N_TOK // T, T])
            per_batch = tables[:].rearrange("p w (b t) -> p w b t", t=T)
            nc.vector.tensor_copy(out=per_batch[:, 1:3, :, :], in_=repeated)
            nc.vector.tensor_scalar(out=per_batch[:, 0, :, :], in0=repeated[:, 1, :, :], scalar1=-1.0, scalar2=None, op0=ALU.mult)
            bank = next_bank()
            nc.tensor.transpose(bank[:, 0:P], bias_rows[:].bitcast(F32), identity[:])
            nc.vector.tensor_copy(out=bias[:], in_=bank[:, 0:PAIRS].bitcast(BF16))

        for position, key in enumerate(order[:prologue_tiles]):
            copy_out(transpose_in(key))
            if position == 1:
                transpose_constants()
            if position < prologue_tiles - 1:
                quantize(key)
            load(order[loaded])
            loaded += 1
        waiting = [order[prologue_tiles - 1]]
        done = prologue_tiles

        rotated = []
        units = [(step, b) for step, (j, first, count) in enumerate(steps) for b in range(count // T)]
        finished = 0
        deferred = []
        first_added_in_psum = len(steps) - 4
        for k in range(len(steps) + 1):
            if k < len(steps):
                j, first, count = steps[k]
                even = project(j, 0, first, count)
                odd = project(j, 1, first, count)
                even_products = times_tables(even, j, 0, count)
                odd_products = times_tables(odd, j, 1, count)
                for key in waiting:
                    quantize(key)
                if k == B - 1:
                    nc.vector.tensor_copy(out=wide_gains[:], in_=gains[:].unsqueeze(2).to_broadcast([P, 2, 4, HD]))
                waiting = order[done : done + tiles_in_step[k]]
                done += tiles_in_step[k]
                if k < first_added_in_psum:
                    halves = work.tile([P, 2, count], F32, name="halves", tag="halves", bufs=LAG + 1)
                    nc.gpsimd.tensor_tensor(out=halves[:], in0=even_products[:], in1=odd_products[:], op=ALU.add)
                    rotated.append([halves])
                else:
                    rotated.append([even_products, odd_products])
            else:
                waiting = []
            for job in deferred:
                normalise(*job)
            deferred = []
            catching_up = k >= len(steps) - 4
            lag = 1 if catching_up else LAG
            due = [unit for unit in units[finished : finished + 3] if unit[0] <= k - lag]
            ready = []
            for step, b in due:
                j, first, count = steps[step]
                ready.append((j, first + b * T, transpose_out(rotated[step], b)))
            copies = transpose_in(waiting[0]) if waiting else []
            sums = [sum_squares(heads) for j, first, heads in ready[:2]]
            roots = []
            for b in range(len(ready)):
                roots.append(inverse_root(sums[b]))
                copy_out(copies[b : b + 1])
                if b + 2 < len(ready):
                    sums.append(sum_squares(ready[b + 2][2]))
            copy_out(copies[len(ready) :])
            for b, (j, first, heads) in enumerate(ready):
                on_scalar = 4 if catching_up else 3
                if b != 1 or finished + b >= len(units) - 4:
                    on_scalar = 0
                if k >= len(steps) - 3:
                    deferred.append((j, first, heads, roots[b], on_scalar, finished + b == len(units) - 1))
                else:
                    normalise(j, first, heads, roots[b], on_scalar, False)
            finished += len(due)
            for key in waiting[1:]:
                copy_out(transpose_in(key))
            for key in waiting:
                if loaded < len(order):
                    load(order[loaded])
                    loaded += 1
        for job in deferred:
            normalise(*job)
        assert finished == len(units)
